import numpy as np
import ml_dtypes


def mxq(x, axis, fmt="e4m3"):
    dtype, down = {"e4m3": (ml_dtypes.float8_e4m3fn, 7), "e5m2": (ml_dtypes.float8_e5m2, 14)}[fmt]
    v = np.moveaxis(np.asarray(x, np.float32).astype(ml_dtypes.bfloat16).astype(np.float64), axis, -1)
    blocks = v.reshape(v.shape[:-1] + (-1, 32))
    amax = np.abs(blocks).max(-1, keepdims=True)
    byte = np.maximum(np.where(amax > 0, np.frexp(amax)[1] - 1 + 127, 0) - down, 1)
    scale = np.exp2(byte - 127.0)
    codes = (blocks / scale).astype(np.float32).astype(dtype).astype(np.float64)
    return np.moveaxis((codes * scale).reshape(v.shape), -1, axis)


BF16 = ml_dtypes.bfloat16


def bf(x):
    return np.asarray(x, np.float32).astype(BF16)


def f64(x):
    return np.asarray(x).astype(np.float64)


B, TQ, TV, H, DH = 2, 2048, 512, 8, 128
D = H * DH


def setup_inputs():
    return {"query": bf(np.random.standard_normal((B, TQ, D))),
            "k": bf(np.random.standard_normal((B, TV, D))),
            "value": bf(np.random.standard_normal((B, TV, DH)) * 0.5)}


def reference(query, k, value):
    qs = f64(query).reshape(B, TQ, H, DH).transpose(0, 2, 1, 3)
    ks = f64(k).reshape(B, TV, H, DH).transpose(0, 2, 3, 1)
    qk = (qs @ ks) * DH ** -0.5
    e = np.exp(qk - qk.max(axis=1, keepdims=True))
    w = e / e.sum(axis=1, keepdims=True)
    ctx = mxq(w, 3, "e4m3") @ mxq(f64(value), 1, "e4m3")[:, None]
    return ctx.transpose(0, 2, 1, 3).reshape(B, TQ, D)

@@ -1,0 +1,379 @@
+from contextlib import ExitStack
+
+import concourse.mybir as mybir
+from concourse.masks import make_identity
+
+F32 = mybir.dt.float32
+BF16 = mybir.dt.bfloat16
+U32 = mybir.dt.uint32
+U8 = mybir.dt.uint8
+FP8X4 = mybir.dt.float8_e4m3fn_x4
+ACTF = mybir.ActivationFunctionType
+ALU = mybir.AluOpType
+AX = mybir.AxisListType
+
+B, TQ, TV, H, DH = 2, 2048, 512, 8, 128
+P = 128
+J = 4
+QB = 64
+NBLK = B * TQ // QB
+NPAIR = NBLK // 2
+BLK_PER_B = TQ // QB
+SCALE = DH ** -0.5
+FLOPS = 2 * 2 * B * H * TQ * TV * DH
+
+GROUPS = [4, 4, 4, 4, 4, 4, 4, 4]
+NE = 12
+QLAG = 2
+MANUAL = True
+
+
+def add(table, step, item):
+    table[step] = table.get(step, []) + [item]
+
+
+def tile_multiheadattention_pa_t_kernel(tc, query, k, value, out):
+    nc = tc.nc
+    with ExitStack() as ctx:
+        const = ctx.enter_context(tc.tile_pool(name="const", bufs=1))
+        work = ctx.enter_context(tc.tile_pool(name="work", bufs=1))
+        psum = ctx.enter_context(tc.psum_pool(name="psum", bufs=1))
+        if MANUAL:
+            ctx.enter_context(tc.manual_schedule())
+
+        identb = const.tile([P, P], BF16, name="identb")
+        identf = const.tile([P, P], F32, name="identf")
+        kt0 = const.tile([P, J, H, P], BF16, name="kt0")
+        kt1 = const.tile([P, J, H, P], BF16, name="kt1")
+        kts = [kt0, kt1]
+        vraw = const.tile([P, B, J, DH], BF16, name="vraw")
+        vg = const.tile([P, B, DH, J], BF16, name="vg", align_bytes=64)
+        vcodes = const.tile([P, B * DH], U32, name="vcodes", align_bytes=64)
+        vplane = const.tile([P, B * DH], U8, name="vplane", align_bytes=64)
+
+        kraw = {}
+        qraw = {}
+        tp = {}
+        qT = {}
+        s = {}
+        m = {}
+        x = {}
+        e = {}
+        st = {}
+        sT = {}
+        lb = {}
+        r = {}
+        w = {}
+        codes = {}
+        planes = {}
+        o = {}
+        osb = {}
+
+        grp_of_pair = {}
+        lb_at = {}
+        ln_at = {}
+        mul_at = {}
+        qz_at = {}
+        mx_at = {}
+        oe_at = {}
+        first = 0
+        next_mul = 0
+        last_step = 0
+        for gi, npg in enumerate(GROUPS):
+            g_last = 2 * (first + npg) - 1
+            add(ln_at, g_last + 2, gi)
+            base = g_last + 3
+            for i in range(npg):
+                grp_of_pair[first + i] = (gi, i, npg)
+                add(lb_at, base + max(0, 2 * i - 1), first + i)
+            for kk in range(2 * npg):
+                stp = max(base + kk, next_mul)
+                next_mul = stp + 1
+                add(mul_at, stp, 2 * first + kk)
+                if kk % 2 == 1:
+                    pair = first + kk // 2
+                    add(qz_at, stp + QLAG, pair)
+                    add(mx_at, stp + QLAG, (pair, 0))
+                    add(oe_at, stp + QLAG + 1, (pair, 0))
+                    add(mx_at, stp + QLAG + 1, (pair, 1))
+                    add(oe_at, stp + QLAG + 2, (pair, 1))
+                    last_step = stp + QLAG + 2
+            first += npg
+        assert first == NPAIR
+
+        ldq_at = {}
+        qtt_at = {}
+        qte_at = {}
+        for qt in range(2, NPAIR):
+            add(ldq_at, max(0, 2 * qt - 7), qt)
+            add(qtt_at, 2 * qt - 3, qt)
+            add(qte_at, 2 * qt - 2, qt)
+        ldk_at = {}
+        ktt_at = {}
+        kte_at = {}
+        for j in range(J):
+            add(ldk_at, j, j)
+            add(ktt_at, 8 + 2 * j, j)
+            add(kte_at, 9 + 2 * j, j)
+
+        def load_k(b, j):
+            if j == 0:
+                t = work.tile([P, J, H * DH], BF16, tag="kraw", bufs=1, name="kraw")
+                kraw[b] = t
+            src = k[b].rearrange("(p j) c -> p j c", j=J)
+            nc.sync.dma_start(out=kraw[b][:, j, :], in_=src[:, j, :])
+
+        def load_q(qt):
+            t = work.tile([P, H * DH], BF16, tag="qraw", bufs=4, name="qraw")
+            qraw[qt] = t
+            b = qt // (NPAIR // B)
+            r0 = (qt % (NPAIR // B)) * P
+            nc.sync.dma_start(out=t[:], in_=query[b, r0:r0 + P, :])
+
+        def k_transpose(b, j, tag, bufs):
+            t = psum.tile([P, H, P], BF16, tag=tag, bufs=bufs, name="ktp")
+            tp[("k", b, j)] = t
+            for h in range(H):
+                nc.tensor.transpose(t[:, h, :], kraw[b][:, j, h * DH:(h + 1) * DH], identb[:])
+
+        def k_evac(b, j):
+            nc.scalar.copy(out=kts[b][:, j, :, :], in_=tp[("k", b, j)][:])
+
+        def q_transpose(qt):
+            t = psum.tile([P, H, P], BF16, tag="tp", bufs=1, name="qtp")
+            tp[("q", qt)] = t
+            for h in range(H):
+                nc.tensor.transpose(t[:, h, :], qraw[qt][:, h * DH:(h + 1) * DH], identb[:])
+
+        def q_evac(qt):
+            t = work.tile([P, H, P], BF16, tag="qT", bufs=3, name="qT")
+            qT[qt] = t
+            nc.scalar.copy(out=t[:], in_=tp[("q", qt)][:])
+
+        def qk(g, j):
+            t = psum.tile([P, H, QB], F32, tag="s", bufs=4, name="s")
+            s[(g, j)] = t
+            b = g // BLK_PER_B
+            half = g % 2
+            for h in range(H):
+                nc.tensor.matmul(
+                    t[:, h, :],
+                    lhsT=kts[b][:, j, h, :],
+                    rhs=qT[g // 2][:, h, half * QB:(half + 1) * QB],
+                    start=True,
+                    stop=True,
+                )
+
+        def red(g, j):
+            if j == 0:
+                t = work.tile([P, J, QB], F32, tag="m", bufs=3, name="m")
+                m[g] = t
+            nc.vector.tensor_reduce(
+                out=m[g][:, j, :],
+                in_=s[(g, j)][:].rearrange("p h q -> p q h"),
+                axis=AX.X,
+                op=ALU.max,
+            )
+
+        def sub(g, j):
+            if j == 0:
+                t = work.tile([P, J, H, QB], F32, tag="x", bufs=3, name="x")
+                x[g] = t
+            nc.vector.tensor_tensor(
+                out=x[g][:, j, :, :],
+                in0=s[(g, j)][:],
+                in1=m[g][:, j, :].unsqueeze(1).to_broadcast([P, H, QB]),
+                op=ALU.subtract,
+            )
+
+        def expo(g):
+            t = work.tile([P, H, QB, J], F32, tag="e", bufs=NE, name="e")
+            e[g] = t
+            nc.scalar.activation(
+                out=t[:],
+                in_=x[g][:].rearrange("p j h q -> p h q j"),
+                func=ACTF.Exp,
+                scale=SCALE,
+            )
+
+        def sumt(g):
+            pair = g // 2
+            half = g % 2
+            if half == 0:
+                t = psum.tile([P, 4, P], F32, tag="st", bufs=1, name="st")
+                st[pair] = t
+            for c in range(2):
+                for h in range(H):
+                    nc.tensor.matmul(
+                        st[pair][:, half * 2 + c, :],
+                        lhsT=e[g][:, h, c * 32:(c + 1) * 32, :].rearrange("p q j -> p (q j)"),
+                        rhs=identf[:],
+                        is_transpose=True,
+                        start=(h == 0),
+                        stop=(h == H - 1),
+                    )
+
+        def st_evac(pair):
+            gi, i, npg = grp_of_pair[pair]
+            if i == 0:
+                t = work.tile([P, 4 * max(GROUPS), P], F32, tag="sT", bufs=2, name="sT")
+                sT[gi] = t
+            nc.scalar.copy(out=sT[gi][:, 4 * i:4 * i + 4, :], in_=st[pair][:])
+
+        def ln(gi):
+            npg = GROUPS[gi]
+            nc.scalar.activation(
+                out=sT[gi][:, 0:4 * npg, :], in_=sT[gi][:, 0:4 * npg, :], func=ACTF.Ln
+            )
+
+        def l_back(pair):
+            gi, i, npg = grp_of_pair[pair]
+            t = psum.tile([P, 4, P], F32, tag="lb", bufs=1, name="lb")
+            lb[pair] = t
+            for c in range(4):
+                nc.tensor.transpose(t[:, c, :], sT[gi][:, 4 * i + c, :], identf[:])
+
+        def rexp(pair):
+            t = work.tile([P, 2, QB * J], F32, tag="r", bufs=3, name="r")
+            r[pair] = t
+            nc.scalar.activation(
+                out=t[:].rearrange("p a c -> p (a c)"),
+                in_=lb[pair][:].rearrange("p a c -> p (a c)"),
+                func=ACTF.Exp,
+                scale=-1.0,
+            )
+
+        def mul(g):
+            pair = g // 2
+            half = g % 2
+            if half == 0:
+                t = work.tile([P, H, P, J], BF16, tag="w", bufs=2, name="w", align_bytes=64)
+                w[pair] = t
+            nc.gpsimd.tensor_tensor(
+                out=w[pair][:, :, half * QB:(half + 1) * QB, :].rearrange("p h q j -> p h (q j)"),
+                in0=e[g][:].rearrange("p h q j -> p h (q j)"),
+                in1=r[pair][:, half, :].unsqueeze(1).to_broadcast([P, H, QB * J]),
+                op=ALU.mult,
+            )
+
+        def quant(pair):
+            c = work.tile([P, H * P], U32, tag="codes", bufs=2, name="codes", align_bytes=64)
+            pl = work.tile([P, H * P], U8, tag="plane", bufs=2, name="plane", align_bytes=64)
+            codes[pair] = c
+            planes[pair] = pl
+            nc.vector.quantize_mx(
+                out=c[:].bitcast(FP8X4),
+                scales=pl[:],
+                in_=w[pair][:].rearrange("p h q j -> p (h q j)"),
+            )
+
+        def mx(pair, hh):
+            t = psum.tile([P, 4, DH], F32, tag="o", bufs=1, name="o")
+            o[(pair, hh)] = t
+            b = pair // (NPAIR // B)
+            for i in range(4):
+                h = hh * 4 + i
+                nc.tensor.matmul_mx(
+                    out=t[:, i, :],
+                    lhsT=codes[pair][:, h * P:(h + 1) * P].bitcast(FP8X4),
+                    lhsT_scale=planes[pair][:, h * P:(h + 1) * P],
+                    rhs=vcodes[:, b * DH:(b + 1) * DH].bitcast(FP8X4),
+                    rhs_scale=vplane[:, b * DH:(b + 1) * DH],
+                    start=True,
+                    stop=True,
+                )
+
+        def o_evac(pair, hh):
+            if hh == 0:
+                t = work.tile([P, H * DH], F32, tag="osb", bufs=2, name="osb")
+                osb[pair] = t
+            nc.scalar.copy(
+                out=osb[pair][:, hh * 512:(hh + 1) * 512],
+                in_=o[(pair, hh)][:].rearrange("p a c -> p (a c)"),
+            )
+            if hh == 1:
+                b = pair // (NPAIR // B)
+                r0 = (pair % (NPAIR // B)) * P
+                nc.sync.dma_start(out=out[b, r0:r0 + P, :], in_=osb[pair][:])
+
+        load_q(0)
+        for j in range(J):
+            load_k(0, j)
+        load_q(1)
+        for b in range(B):
+            nc.sync.dma_start(
+                out=vraw[:, b, :, :], in_=value[b].rearrange("(p j) d -> p j d", j=J)
+            )
+        make_identity(nc, identb[:])
+        make_identity(nc, identf[:])
+        q_transpose(0)
+        q_evac(0)
+        for j in range(J):
+            k_transpose(0, j, "s", 4)
+            k_evac(0, j)
+        q_transpose(1)
+        q_evac(1)
+        nc.vector.tensor_copy(out=vg[:], in_=vraw[:].rearrange("p b j d -> p b d j"))
+        nc.vector.quantize_mx(
+            out=vcodes[:].bitcast(FP8X4),
+            scales=vplane[:],
+            in_=vg[:].rearrange("p b d j -> p (b d j)"),
+        )
+        for j in range(J):
+            qk(0, j)
+
+        for tau in range(last_step + 1):
+            for qt in ldq_at.get(tau, []):
+                load_q(qt)
+            for j in ldk_at.get(tau, []):
+                load_k(1, j)
+            if 0 <= tau - 2 < NBLK:
+                sumt(tau - 2)
+            for pair in lb_at.get(tau, []):
+                l_back(pair)
+            for pair in lb_at.get(tau, []):
+                rexp(pair)
+            for pair, hh in oe_at.get(tau, []):
+                o_evac(pair, hh)
+            for qt in qte_at.get(tau, []):
+                q_evac(qt)
+            for j in kte_at.get(tau, []):
+                k_evac(1, j)
+            for g in mul_at.get(tau, []):
+                mul(g)
+            if 0 <= tau - 1 < NBLK:
+                expo(tau - 1)
+            for pair in qz_at.get(tau, []):
+                quant(pair)
+            has = tau < NBLK
+            nxt = tau + 1 < NBLK
+            if has:
+                red(tau, 0)
+                red(tau, 1)
+                sub(tau, 0)
+            if nxt:
+                qk(tau + 1, 0)
+            for pair, hh in mx_at.get(tau, []):
+                mx(pair, hh)
+            if has:
+                red(tau, 2)
+                sub(tau, 1)
+            if nxt:
+                qk(tau + 1, 1)
+            for qt in qtt_at.get(tau, []):
+                q_transpose(qt)
+            for j in ktt_at.get(tau, []):
+                k_transpose(1, j, "tp", 1)
+            if has:
+                red(tau, 3)
+                sub(tau, 2)
+            if nxt:
+                qk(tau + 1, 2)
+            if has:
+                sub(tau, 3)
+            if nxt:
+                qk(tau + 1, 3)
+            if 0 <= tau - 2 < NBLK and (tau - 2) % 2 == 1:
+                st_evac((tau - 2) // 2)
+            for gi in ln_at.get(tau, []):
+                ln(gi)

@@ -22,10 +22,14 @@ BLK_PER_B = TQ // QB
 SCALE = DH ** -0.5
 FLOPS = 2 * 2 * B * H * TQ * TV * DH
 
-GROUPS = [4, 4, 4, 4, 4, 4, 4, 4]
+GROUPS = [4, 4, 4, 4, 4, 4, 3, 2, 3]
 NE = 12
-QLAG = 2
+QLAG = 1
 MANUAL = True
+MUL_PIECES = 1
+WBUFS = 1
+QPOS = 4
+FIRST_V = 54
 
 
 def add(table, step, item):
@@ -86,18 +90,20 @@ def tile_multiheadattention_pa_t_kernel(tc, query, k, value, out):
             for i in range(npg):
                 grp_of_pair[first + i] = (gi, i, npg)
                 add(lb_at, base + max(0, 2 * i - 1), first + i)
-            for kk in range(2 * npg):
-                stp = max(base + kk, next_mul)
-                next_mul = stp + 1
-                add(mul_at, stp, 2 * first + kk)
-                if kk % 2 == 1:
-                    pair = first + kk // 2
-                    add(qz_at, stp + QLAG, pair)
-                    add(mx_at, stp + QLAG, (pair, 0))
-                    add(oe_at, stp + QLAG + 1, (pair, 0))
-                    add(mx_at, stp + QLAG + 1, (pair, 1))
-                    add(oe_at, stp + QLAG + 2, (pair, 1))
-                    last_step = stp + QLAG + 2
+            for i in range(npg):
+                pair = first + i
+                if 2 * pair < FIRST_V:
+                    stp = max(base + 2 * i, next_mul)
+                    next_mul = stp + 2
+                    add(mul_at, stp, 2 * pair)
+                    add(mul_at, stp + 1, 2 * pair + 1)
+                    stq = stp + 1 + QLAG
+                    add(qz_at, stq, pair)
+                    add(mx_at, stq + 1, (pair, 0))
+                    add(oe_at, stq + 2, (pair, 0))
+                    add(mx_at, stq + 2, (pair, 1))
+                    add(oe_at, stq + 3, (pair, 1))
+                    last_step = max(last_step, stq + 3)
             first += npg
         assert first == NPAIR
 
@@ -226,15 +232,15 @@ def tile_multiheadattention_pa_t_kernel(tc, query, k, value, out):
                 out=sT[gi][:, 0:4 * npg, :], in_=sT[gi][:, 0:4 * npg, :], func=ACTF.Ln
             )
 
-        def l_back(pair):
+        def l_back(pair, tag="lb"):
             gi, i, npg = grp_of_pair[pair]
-            t = psum.tile([P, 4, P], F32, tag="lb", bufs=1, name="lb")
+            t = psum.tile([P, 4, P], F32, tag=tag, bufs=1, name="lb")
             lb[pair] = t
             for c in range(4):
                 nc.tensor.transpose(t[:, c, :], sT[gi][:, 4 * i + c, :], identf[:])
 
         def rexp(pair):
-            t = work.tile([P, 2, QB * J], F32, tag="r", bufs=3, name="r")
+            t = work.tile([P, 2, QB * J], F32, tag="r", bufs=6, name="r")
             r[pair] = t
             nc.scalar.activation(
                 out=t[:].rearrange("p a c -> p (a c)"),
@@ -247,14 +253,27 @@ def tile_multiheadattention_pa_t_kernel(tc, query, k, value, out):
             pair = g // 2
             half = g % 2
             if half == 0:
-                t = work.tile([P, H, P, J], BF16, tag="w", bufs=2, name="w", align_bytes=64)
+                t = work.tile(
+                    [P, H, P, J],
+                    BF16,
+                    tag="wv" if g >= FIRST_V else "w",
+                    bufs=WBUFS,
+                    name="w",
+                    align_bytes=64,
+                )
                 w[pair] = t
-            nc.gpsimd.tensor_tensor(
-                out=w[pair][:, :, half * QB:(half + 1) * QB, :].rearrange("p h q j -> p h (q j)"),
-                in0=e[g][:].rearrange("p h q j -> p h (q j)"),
-                in1=r[pair][:, half, :].unsqueeze(1).to_broadcast([P, H, QB * J]),
-                op=ALU.mult,
-            )
+            eng = nc.vector if g >= FIRST_V else nc.gpsimd
+            npc = 1 if g >= FIRST_V else MUL_PIECES
+            hp = H // npc
+            for pc in range(npc):
+                eng.tensor_tensor(
+                    out=w[pair][:, pc * hp:(pc + 1) * hp, half * QB:(half + 1) * QB, :].rearrange(
+                        "p h q j -> p h (q j)"
+                    ),
+                    in0=e[g][:, pc * hp:(pc + 1) * hp, :, :].rearrange("p h q j -> p h (q j)"),
+                    in1=r[pair][:, half, :].unsqueeze(1).to_broadcast([P, hp, QB * J]),
+                    op=ALU.mult,
+                )
 
         def quant(pair):
             c = work.tile([P, H * P], U32, tag="codes", bufs=2, name="codes", align_bytes=64)
@@ -267,8 +286,8 @@ def tile_multiheadattention_pa_t_kernel(tc, query, k, value, out):
                 in_=w[pair][:].rearrange("p h q j -> p (h q j)"),
             )
 
-        def mx(pair, hh):
-            t = psum.tile([P, 4, DH], F32, tag="o", bufs=1, name="o")
+        def mx(pair, hh, tag="o", bufs=1):
+            t = psum.tile([P, 4, DH], F32, tag=tag, bufs=bufs, name="o")
             o[(pair, hh)] = t
             b = pair // (NPAIR // B)
             for i in range(4):
@@ -322,58 +341,109 @@ def tile_multiheadattention_pa_t_kernel(tc, query, k, value, out):
         for j in range(J):
             qk(0, j)
 
-        for tau in range(last_step + 1):
+        for tau in range(NBLK):
             for qt in ldq_at.get(tau, []):
                 load_q(qt)
             for j in ldk_at.get(tau, []):
                 load_k(1, j)
-            if 0 <= tau - 2 < NBLK:
-                sumt(tau - 2)
             for pair in lb_at.get(tau, []):
                 l_back(pair)
-            for pair in lb_at.get(tau, []):
-                rexp(pair)
+            if 0 <= tau - 2 < NBLK:
+                sumt(tau - 2)
             for pair, hh in oe_at.get(tau, []):
                 o_evac(pair, hh)
             for qt in qte_at.get(tau, []):
                 q_evac(qt)
             for j in kte_at.get(tau, []):
                 k_evac(1, j)
-            for g in mul_at.get(tau, []):
-                mul(g)
+            for pair in lb_at.get(tau, []):
+                rexp(pair)
             if 0 <= tau - 1 < NBLK:
                 expo(tau - 1)
-            for pair in qz_at.get(tau, []):
-                quant(pair)
             has = tau < NBLK
             nxt = tau + 1 < NBLK
+
+            def slot(i):
+                if i == QPOS:
+                    for pair in qz_at.get(tau, []):
+                        quant(pair)
+                    for g in mul_at.get(tau, []):
+                        mul(g)
+                if i == 1:
+                    for pair, hh in mx_at.get(tau, []):
+                        mx(pair, hh)
+                if i == 2:
+                    for qt in qtt_at.get(tau, []):
+                        q_transpose(qt)
+                    for j in ktt_at.get(tau, []):
+                        k_transpose(1, j, "tp", 1)
+
+            slot(0)
             if has:
                 red(tau, 0)
                 red(tau, 1)
                 sub(tau, 0)
             if nxt:
                 qk(tau + 1, 0)
-            for pair, hh in mx_at.get(tau, []):
-                mx(pair, hh)
+            slot(1)
             if has:
                 red(tau, 2)
                 sub(tau, 1)
             if nxt:
                 qk(tau + 1, 1)
-            for qt in qtt_at.get(tau, []):
-                q_transpose(qt)
-            for j in ktt_at.get(tau, []):
-                k_transpose(1, j, "tp", 1)
+            slot(2)
             if has:
                 red(tau, 3)
                 sub(tau, 2)
             if nxt:
                 qk(tau + 1, 2)
+            slot(3)
             if has:
                 sub(tau, 3)
             if nxt:
                 qk(tau + 1, 3)
+            slot(4)
             if 0 <= tau - 2 < NBLK and (tau - 2) % 2 == 1:
                 st_evac((tau - 2) // 2)
             for gi in ln_at.get(tau, []):
                 ln(gi)
+
+        def mul_quant(pair):
+            mul(2 * pair)
+            mul(2 * pair + 1)
+            quant(pair)
+
+        def mx_both(pair):
+            mx(pair, 0, "s", 4)
+            mx(pair, 1, "s", 4)
+
+        def evac_both(pair):
+            o_evac(pair, 0)
+            o_evac(pair, 1)
+
+        pv = FIRST_V // 2
+        assert last_step == NBLK + 3 and GROUPS[-1] == 3 and pv == NPAIR - 5
+        o_evac(pv - 2, 0)
+        mx(pv - 2, 1)
+        sumt(NBLK - 2)
+        expo(NBLK - 1)
+        quant(pv - 1)
+        mul_quant(pv)
+        sumt(NBLK - 1)
+        o_evac(pv - 2, 1)
+        mx_both(pv - 1)
+        st_evac(NPAIR - 1)
+        ln(len(GROUPS) - 1)
+        l_back(NPAIR - 3, "lb")
+        l_back(NPAIR - 2, "tp")
+        rexp(NPAIR - 3)
+        l_back(NPAIR - 1, "lb")
+        rexp(NPAIR - 2)
+        rexp(NPAIR - 1)
+        evac_both(pv - 1)
+        mx_both(pv)
+        for pair in range(pv + 1, NPAIR):
+            mul_quant(pair)
+            evac_both(pair - 1)
+            mx_both(pair)
+        evac_both(NPAIR - 1)

@@ -22,14 +22,14 @@ BLK_PER_B = TQ // QB
 SCALE = DH ** -0.5
 FLOPS = 2 * 2 * B * H * TQ * TV * DH
 
-GROUPS = [4, 4, 4, 4, 4, 4, 3, 2, 3]
-NE = 12
+GROUPS = [3, 3, 3, 3, 3, 3, 3, 3, 3, 2, 3]
+NE = 11
 QLAG = 1
 MANUAL = True
 MUL_PIECES = 1
 WBUFS = 1
 QPOS = 4
-FIRST_V = 54
+FIRST_V = 55
 
 
 def add(table, step, item):
@@ -96,6 +96,7 @@ def tile_multiheadattention_pa_t_kernel(tc, query, k, value, out):
                     stp = max(base + 2 * i, next_mul)
                     next_mul = stp + 2
                     add(mul_at, stp, 2 * pair)
+                if 2 * pair + 1 < FIRST_V:
                     add(mul_at, stp + 1, 2 * pair + 1)
                     stq = stp + 1 + QLAG
                     add(qz_at, stq, pair)
@@ -232,6 +233,16 @@ def tile_multiheadattention_pa_t_kernel(tc, query, k, value, out):
                 out=sT[gi][:, 0:4 * npg, :], in_=sT[gi][:, 0:4 * npg, :], func=ACTF.Ln
             )
 
+        def ln_end():
+            gi = len(GROUPS) - 1
+            npg = GROUPS[gi]
+            nc.scalar.activation(
+                out=sT[gi][:, 0:4 * npg - 4, :], in_=sT[gi][:, 0:4 * npg - 4, :], func=ACTF.Ln
+            )
+            nc.scalar.activation(
+                out=sT[gi][:, 4 * npg - 4:4 * npg, :], in_=st[NPAIR - 1][:], func=ACTF.Ln
+            )
+
         def l_back(pair, tag="lb"):
             gi, i, npg = grp_of_pair[pair]
             t = psum.tile([P, 4, P], F32, tag=tag, bufs=1, name="lb")
@@ -302,17 +313,21 @@ def tile_multiheadattention_pa_t_kernel(tc, query, k, value, out):
                     stop=True,
                 )
 
-        def o_evac(pair, hh):
+        def o_evac(pair, hh, last=False):
             if hh == 0:
                 t = work.tile([P, H * DH], F32, tag="osb", bufs=2, name="osb")
                 osb[pair] = t
-            nc.scalar.copy(
-                out=osb[pair][:, hh * 512:(hh + 1) * 512],
-                in_=o[(pair, hh)][:].rearrange("p a c -> p (a c)"),
-            )
-            if hh == 1:
-                b = pair // (NPAIR // B)
-                r0 = (pair % (NPAIR // B)) * P
+            cols = slice(hh * 512, (hh + 1) * 512)
+            src = o[(pair, hh)][:].rearrange("p a c -> p (a c)")
+            b = pair // (NPAIR // B)
+            r0 = (pair % (NPAIR // B)) * P
+            if last and hh == 1:
+                nc.vector.tensor_copy(out=osb[pair][:, cols], in_=src)
+            else:
+                nc.scalar.copy(out=osb[pair][:, cols], in_=src)
+            if last:
+                nc.sync.dma_start(out=out[b, r0:r0 + P, cols], in_=osb[pair][:, cols])
+            elif hh == 1:
                 nc.sync.dma_start(out=out[b, r0:r0 + P, :], in_=osb[pair][:])
 
         load_q(0)
@@ -326,10 +341,14 @@ def tile_multiheadattention_pa_t_kernel(tc, query, k, value, out):
         make_identity(nc, identb[:])
         make_identity(nc, identf[:])
         q_transpose(0)
+        k_transpose(0, 0, "st", 1)
+        k_transpose(0, 1, "lb", 1)
+        k_transpose(0, 2, "o", 1)
         q_evac(0)
+        k_transpose(0, 3, "tp", 1)
         for j in range(J):
-            k_transpose(0, j, "s", 4)
             k_evac(0, j)
+            qk(0, j)
         q_transpose(1)
         q_evac(1)
         nc.vector.tensor_copy(out=vg[:], in_=vraw[:].rearrange("p b j d -> p b d j"))
@@ -338,8 +357,6 @@ def tile_multiheadattention_pa_t_kernel(tc, query, k, value, out):
             scales=vplane[:],
             in_=vg[:].rearrange("p b d j -> p (b d j)"),
         )
-        for j in range(J):
-            qk(0, j)
 
         for tau in range(NBLK):
             for qt in ldq_at.get(tau, []):
@@ -421,19 +438,19 @@ def tile_multiheadattention_pa_t_kernel(tc, query, k, value, out):
             o_evac(pair, 0)
             o_evac(pair, 1)
 
-        pv = FIRST_V // 2
-        assert last_step == NBLK + 3 and GROUPS[-1] == 3 and pv == NPAIR - 5
+        pv = (FIRST_V + 1) // 2
+        assert FIRST_V % 2 == 1 and last_step == NBLK + 1 and GROUPS[-1] == 3 and pv <= NPAIR - 4
         o_evac(pv - 2, 0)
         mx(pv - 2, 1)
         sumt(NBLK - 2)
         expo(NBLK - 1)
+        mul(FIRST_V)
         quant(pv - 1)
         mul_quant(pv)
         sumt(NBLK - 1)
         o_evac(pv - 2, 1)
         mx_both(pv - 1)
-        st_evac(NPAIR - 1)
-        ln(len(GROUPS) - 1)
+        ln_end()
         l_back(NPAIR - 3, "lb")
         l_back(NPAIR - 2, "tp")
         rexp(NPAIR - 3)
@@ -446,4 +463,5 @@ def tile_multiheadattention_pa_t_kernel(tc, query, k, value, out):
             mul_quant(pair)
             evac_both(pair - 1)
             mx_both(pair)
-        evac_both(NPAIR - 1)
+        o_evac(NPAIR - 1, 0, True)
+        o_evac(NPAIR - 1, 1, True)

@@ -8,32 +8,39 @@ BF16 = mybir.dt.bfloat16
 U32 = mybir.dt.uint32
 U8 = mybir.dt.uint8
 FP8X4 = mybir.dt.float8_e4m3fn_x4
-ACTF = mybir.ActivationFunctionType
+ACT = mybir.ActivationFunctionType
 ALU = mybir.AluOpType
 AX = mybir.AxisListType
 
 B, TQ, TV, H, DH = 2, 2048, 512, 8, 128
-P = 128
-J = 4
-QB = 64
-NBLK = B * TQ // QB
-NPAIR = NBLK // 2
-BLK_PER_B = TQ // QB
-SCALE = DH ** -0.5
 FLOPS = 2 * 2 * B * H * TQ * TV * DH
 
-GROUPS = [3, 3, 3, 3, 3, 3, 3, 3, 3, 2, 3]
-NE = 11
-QLAG = 1
-MANUAL = True
-MUL_PIECES = 1
-WBUFS = 1
-QPOS = 4
-FIRST_V = 55
+P = 128
+J = TV // P
+HALF = 64
+N_HALF = B * TQ // HALF
+N_QT = N_HALF // 2
+QT_PER_B = N_QT // B
+WORD_COLS = HALF * J
+SCALE = DH ** -0.5
+
+GROUP = 3
+QT_VECTOR = N_QT - 5
+
+LOAD_Q = -7
+TRANSPOSE_Q = -3
+COPY_Q = -2
+WEIGHTS = 2 * GROUP + 2
+QUANTISE = WEIGHTS + 2
+CONTEXT = QUANTISE + 1
+COPY_OUT = CONTEXT + 1
+K1_FIRST = 8
+FIRST_LOADS = 4
 
 
-def add(table, step, item):
-    table[step] = table.get(step, []) + [item]
+def due(step, offset):
+    qt, odd = divmod(step - offset, 2)
+    return qt if odd == 0 and 0 <= qt < N_QT else -1
 
 
 def tile_multiheadattention_pa_t_kernel(tc, query, k, value, out):
@@ -42,426 +49,303 @@ def tile_multiheadattention_pa_t_kernel(tc, query, k, value, out):
         const = ctx.enter_context(tc.tile_pool(name="const", bufs=1))
         work = ctx.enter_context(tc.tile_pool(name="work", bufs=1))
         psum = ctx.enter_context(tc.psum_pool(name="psum", bufs=1))
-        if MANUAL:
-            ctx.enter_context(tc.manual_schedule())
+        ctx.enter_context(tc.manual_schedule())
 
-        identb = const.tile([P, P], BF16, name="identb")
-        identf = const.tile([P, P], F32, name="identf")
-        kt0 = const.tile([P, J, H, P], BF16, name="kt0")
-        kt1 = const.tile([P, J, H, P], BF16, name="kt1")
-        kts = [kt0, kt1]
-        vraw = const.tile([P, B, J, DH], BF16, name="vraw")
-        vg = const.tile([P, B, DH, J], BF16, name="vg", align_bytes=64)
-        vcodes = const.tile([P, B * DH], U32, name="vcodes", align_bytes=64)
-        vplane = const.tile([P, B * DH], U8, name="vplane", align_bytes=64)
+        ident_bf = const.tile([P, P], BF16, name="ident_bf")
+        ident_f = const.tile([P, P], F32, name="ident_f")
+        kT = [const.tile([P, J, H, P], BF16, name="kT%d" % b) for b in range(B)]
+        v_raw = const.tile([P, B, J, DH], BF16, name="v_raw")
+        v_words = const.tile([P, B, DH, J], BF16, name="v_words", align_bytes=64)
+        v_codes = const.tile([P, B * DH], U32, name="v_codes", align_bytes=64)
+        v_scales = const.tile([P, B * DH], U8, name="v_scales", align_bytes=64)
 
-        kraw = {}
-        qraw = {}
-        tp = {}
-        qT = {}
-        s = {}
-        m = {}
-        x = {}
-        e = {}
-        st = {}
-        sT = {}
-        lb = {}
-        r = {}
-        w = {}
-        codes = {}
-        planes = {}
-        o = {}
-        osb = {}
+        k_raw, q_raw, turned, qT = {}, {}, {}, {}
+        s, top, x, e = {}, {}, {}, {}
+        sumT, logT, log, inv = {}, {}, {}, {}
+        w, codes, scales, ctx_ps, out_sb = {}, {}, {}, {}, {}
 
-        grp_of_pair = {}
-        lb_at = {}
-        ln_at = {}
-        mul_at = {}
-        qz_at = {}
-        mx_at = {}
-        oe_at = {}
-        first = 0
-        next_mul = 0
-        last_step = 0
-        for gi, npg in enumerate(GROUPS):
-            g_last = 2 * (first + npg) - 1
-            add(ln_at, g_last + 2, gi)
-            base = g_last + 3
-            for i in range(npg):
-                grp_of_pair[first + i] = (gi, i, npg)
-                add(lb_at, base + max(0, 2 * i - 1), first + i)
-            for i in range(npg):
-                pair = first + i
-                if 2 * pair < FIRST_V:
-                    stp = max(base + 2 * i, next_mul)
-                    next_mul = stp + 2
-                    add(mul_at, stp, 2 * pair)
-                if 2 * pair + 1 < FIRST_V:
-                    add(mul_at, stp + 1, 2 * pair + 1)
-                    stq = stp + 1 + QLAG
-                    add(qz_at, stq, pair)
-                    add(mx_at, stq + 1, (pair, 0))
-                    add(oe_at, stq + 2, (pair, 0))
-                    add(mx_at, stq + 2, (pair, 1))
-                    add(oe_at, stq + 3, (pair, 1))
-                    last_step = max(last_step, stq + 3)
-            first += npg
-        assert first == NPAIR
-
-        ldq_at = {}
-        qtt_at = {}
-        qte_at = {}
-        for qt in range(2, NPAIR):
-            add(ldq_at, max(0, 2 * qt - 7), qt)
-            add(qtt_at, 2 * qt - 3, qt)
-            add(qte_at, 2 * qt - 2, qt)
-        ldk_at = {}
-        ktt_at = {}
-        kte_at = {}
-        for j in range(J):
-            add(ldk_at, j, j)
-            add(ktt_at, 8 + 2 * j, j)
-            add(kte_at, 9 + 2 * j, j)
+        def rows(qt):
+            return qt // QT_PER_B, slice((qt % QT_PER_B) * P, (qt % QT_PER_B + 1) * P)
 
         def load_k(b, j):
             if j == 0:
-                t = work.tile([P, J, H * DH], BF16, tag="kraw", bufs=1, name="kraw")
-                kraw[b] = t
-            src = k[b].rearrange("(p j) c -> p j c", j=J)
-            nc.sync.dma_start(out=kraw[b][:, j, :], in_=src[:, j, :])
+                k_raw[b] = work.tile([P, J, H * DH], BF16, tag="k_raw", name="k_raw")
+            nc.sync.dma_start(
+                out=k_raw[b][:, j, :], in_=k[b].rearrange("(p j) c -> p j c", j=J)[:, j, :]
+            )
 
         def load_q(qt):
-            t = work.tile([P, H * DH], BF16, tag="qraw", bufs=4, name="qraw")
-            qraw[qt] = t
-            b = qt // (NPAIR // B)
-            r0 = (qt % (NPAIR // B)) * P
-            nc.sync.dma_start(out=t[:], in_=query[b, r0:r0 + P, :])
+            b, r = rows(qt)
+            q_raw[qt] = work.tile([P, H * DH], BF16, tag="q_raw", bufs=4, name="q_raw")
+            nc.sync.dma_start(out=q_raw[qt][:], in_=query[b, r, :])
 
-        def k_transpose(b, j, tag, bufs):
-            t = psum.tile([P, H, P], BF16, tag=tag, bufs=bufs, name="ktp")
-            tp[("k", b, j)] = t
+        def transpose_heads(key, src, tag):
+            turned[key] = psum.tile([P, H, P], BF16, tag=tag, name="turned")
             for h in range(H):
-                nc.tensor.transpose(t[:, h, :], kraw[b][:, j, h * DH:(h + 1) * DH], identb[:])
+                nc.tensor.transpose(
+                    turned[key][:, h, :], src[:, h * DH:(h + 1) * DH], ident_bf[:]
+                )
 
-        def k_evac(b, j):
-            nc.scalar.copy(out=kts[b][:, j, :, :], in_=tp[("k", b, j)][:])
+        def copy_k(b, j):
+            nc.scalar.copy(out=kT[b][:, j, :, :], in_=turned[("k", b, j)][:])
 
-        def q_transpose(qt):
-            t = psum.tile([P, H, P], BF16, tag="tp", bufs=1, name="qtp")
-            tp[("q", qt)] = t
-            for h in range(H):
-                nc.tensor.transpose(t[:, h, :], qraw[qt][:, h * DH:(h + 1) * DH], identb[:])
+        def copy_q(qt):
+            qT[qt] = work.tile([P, H, P], BF16, tag="qT", bufs=3, name="qT")
+            nc.scalar.copy(out=qT[qt][:], in_=turned[("q", qt)][:])
 
-        def q_evac(qt):
-            t = work.tile([P, H, P], BF16, tag="qT", bufs=3, name="qT")
-            qT[qt] = t
-            nc.scalar.copy(out=t[:], in_=tp[("q", qt)][:])
-
-        def qk(g, j):
-            t = psum.tile([P, H, QB], F32, tag="s", bufs=4, name="s")
-            s[(g, j)] = t
-            b = g // BLK_PER_B
-            half = g % 2
+        def scores(hf, j):
+            s[(hf, j)] = psum.tile([P, H, HALF], F32, tag="s", bufs=4, name="s")
+            side = hf % 2
             for h in range(H):
                 nc.tensor.matmul(
-                    t[:, h, :],
-                    lhsT=kts[b][:, j, h, :],
-                    rhs=qT[g // 2][:, h, half * QB:(half + 1) * QB],
+                    s[(hf, j)][:, h, :],
+                    lhsT=kT[hf // (N_HALF // B)][:, j, h, :],
+                    rhs=qT[hf // 2][:, h, side * HALF:(side + 1) * HALF],
                     start=True,
                     stop=True,
                 )
 
-        def red(g, j):
+        def head_max(hf, j):
             if j == 0:
-                t = work.tile([P, J, QB], F32, tag="m", bufs=3, name="m")
-                m[g] = t
+                top[hf] = work.tile([P, J, HALF], F32, tag="top", bufs=3, name="top")
             nc.vector.tensor_reduce(
-                out=m[g][:, j, :],
-                in_=s[(g, j)][:].rearrange("p h q -> p q h"),
+                out=top[hf][:, j, :],
+                in_=s[(hf, j)][:].rearrange("p h q -> p q h"),
                 axis=AX.X,
                 op=ALU.max,
             )
 
-        def sub(g, j):
+        def shift(hf, j):
             if j == 0:
-                t = work.tile([P, J, H, QB], F32, tag="x", bufs=3, name="x")
-                x[g] = t
+                x[hf] = work.tile([P, J, H, HALF], F32, tag="x", bufs=3, name="x")
             nc.vector.tensor_tensor(
-                out=x[g][:, j, :, :],
-                in0=s[(g, j)][:],
-                in1=m[g][:, j, :].unsqueeze(1).to_broadcast([P, H, QB]),
+                out=x[hf][:, j, :, :],
+                in0=s[(hf, j)][:],
+                in1=top[hf][:, j, :].unsqueeze(1).to_broadcast([P, H, HALF]),
                 op=ALU.subtract,
             )
 
-        def expo(g):
-            t = work.tile([P, H, QB, J], F32, tag="e", bufs=NE, name="e")
-            e[g] = t
+        def exponent(hf):
+            if hf % 2 == 0:
+                e[hf // 2] = work.tile([P, 2, H, HALF, J], F32, tag="e", bufs=6, name="e")
             nc.scalar.activation(
-                out=t[:],
-                in_=x[g][:].rearrange("p j h q -> p h q j"),
-                func=ACTF.Exp,
+                out=e[hf // 2][:, hf % 2, :, :, :],
+                in_=x[hf][:].rearrange("p j h q -> p h q j"),
+                func=ACT.Exp,
                 scale=SCALE,
             )
 
-        def sumt(g):
-            pair = g // 2
-            half = g % 2
-            if half == 0:
-                t = psum.tile([P, 4, P], F32, tag="st", bufs=1, name="st")
-                st[pair] = t
+        def head_sum(hf):
+            qt, side = divmod(hf, 2)
+            if side == 0:
+                sumT[qt] = psum.tile([P, 4, P], F32, tag="sum", name="sumT")
             for c in range(2):
                 for h in range(H):
                     nc.tensor.matmul(
-                        st[pair][:, half * 2 + c, :],
-                        lhsT=e[g][:, h, c * 32:(c + 1) * 32, :].rearrange("p q j -> p (q j)"),
-                        rhs=identf[:],
+                        sumT[qt][:, 2 * side + c, :],
+                        lhsT=e[qt][:, side, h, c * 32:(c + 1) * 32, :].rearrange(
+                            "p q j -> p (q j)"
+                        ),
+                        rhs=ident_f[:],
                         is_transpose=True,
                         start=(h == 0),
                         stop=(h == H - 1),
                     )
 
-        def st_evac(pair):
-            gi, i, npg = grp_of_pair[pair]
-            if i == 0:
-                t = work.tile([P, 4 * max(GROUPS), P], F32, tag="sT", bufs=2, name="sT")
-                sT[gi] = t
-            nc.scalar.copy(out=sT[gi][:, 4 * i:4 * i + 4, :], in_=st[pair][:])
+        def copy_sum(qt):
+            if qt % GROUP == 0:
+                logT[qt // GROUP] = work.tile(
+                    [P, GROUP, 4, P], F32, tag="logT", bufs=2, name="logT"
+                )
+            nc.scalar.copy(out=logT[qt // GROUP][:, qt % GROUP, :, :], in_=sumT[qt][:])
 
-        def ln(gi):
-            npg = GROUPS[gi]
-            nc.scalar.activation(
-                out=sT[gi][:, 0:4 * npg, :], in_=sT[gi][:, 0:4 * npg, :], func=ACTF.Ln
-            )
+        def log_sum(group, n_qt):
+            part = logT[group][:, 0:n_qt, :, :]
+            nc.scalar.activation(out=part, in_=part, func=ACT.Ln)
 
-        def ln_end():
-            gi = len(GROUPS) - 1
-            npg = GROUPS[gi]
-            nc.scalar.activation(
-                out=sT[gi][:, 0:4 * npg - 4, :], in_=sT[gi][:, 0:4 * npg - 4, :], func=ACTF.Ln
-            )
-            nc.scalar.activation(
-                out=sT[gi][:, 4 * npg - 4:4 * npg, :], in_=st[NPAIR - 1][:], func=ACTF.Ln
-            )
-
-        def l_back(pair, tag="lb"):
-            gi, i, npg = grp_of_pair[pair]
-            t = psum.tile([P, 4, P], F32, tag=tag, bufs=1, name="lb")
-            lb[pair] = t
+        def log_back(qt, tag="log"):
+            log[qt] = psum.tile([P, 4, P], F32, tag=tag, name="log")
             for c in range(4):
-                nc.tensor.transpose(t[:, c, :], sT[gi][:, 4 * i + c, :], identf[:])
+                nc.tensor.transpose(
+                    log[qt][:, c, :], logT[qt // GROUP][:, qt % GROUP, c, :], ident_f[:]
+                )
 
-        def rexp(pair):
-            t = work.tile([P, 2, QB * J], F32, tag="r", bufs=6, name="r")
-            r[pair] = t
+        def inverse(qt):
+            inv[qt] = work.tile([P, 2, WORD_COLS], F32, tag="inv", bufs=4, name="inv")
             nc.scalar.activation(
-                out=t[:].rearrange("p a c -> p (a c)"),
-                in_=lb[pair][:].rearrange("p a c -> p (a c)"),
-                func=ACTF.Exp,
+                out=inv[qt][:].rearrange("p a c -> p (a c)"),
+                in_=log[qt][:].rearrange("p a c -> p (a c)"),
+                func=ACT.Exp,
                 scale=-1.0,
             )
 
-        def mul(g):
-            pair = g // 2
-            half = g % 2
-            if half == 0:
-                t = work.tile(
-                    [P, H, P, J],
-                    BF16,
-                    tag="wv" if g >= FIRST_V else "w",
-                    bufs=WBUFS,
-                    name="w",
-                    align_bytes=64,
-                )
-                w[pair] = t
-            eng = nc.vector if g >= FIRST_V else nc.gpsimd
-            npc = 1 if g >= FIRST_V else MUL_PIECES
-            hp = H // npc
-            for pc in range(npc):
-                eng.tensor_tensor(
-                    out=w[pair][:, pc * hp:(pc + 1) * hp, half * QB:(half + 1) * QB, :].rearrange(
-                        "p h q j -> p h (q j)"
-                    ),
-                    in0=e[g][:, pc * hp:(pc + 1) * hp, :, :].rearrange("p h q j -> p h (q j)"),
-                    in1=r[pair][:, half, :].unsqueeze(1).to_broadcast([P, hp, QB * J]),
-                    op=ALU.mult,
-                )
-
-        def quant(pair):
-            c = work.tile([P, H * P], U32, tag="codes", bufs=2, name="codes", align_bytes=64)
-            pl = work.tile([P, H * P], U8, tag="plane", bufs=2, name="plane", align_bytes=64)
-            codes[pair] = c
-            planes[pair] = pl
-            nc.vector.quantize_mx(
-                out=c[:].bitcast(FP8X4),
-                scales=pl[:],
-                in_=w[pair][:].rearrange("p h q j -> p (h q j)"),
+        def weights(qt, engine):
+            w[qt] = work.tile([P, H, P, J], BF16, tag="w", name="w", align_bytes=64)
+            engine.tensor_tensor(
+                out=w[qt][:].rearrange("p h (a q) j -> p h a (q j)", a=2),
+                in0=e[qt][:].rearrange("p a h q j -> p h a (q j)"),
+                in1=inv[qt][:].unsqueeze(1).to_broadcast([P, H, 2, WORD_COLS]),
+                op=ALU.mult,
             )
 
-        def mx(pair, hh, tag="o", bufs=1):
-            t = psum.tile([P, 4, DH], F32, tag=tag, bufs=bufs, name="o")
-            o[(pair, hh)] = t
-            b = pair // (NPAIR // B)
+        def quantise(qt):
+            codes[qt] = work.tile([P, H * P], U32, tag="codes", bufs=2, name="codes", align_bytes=64)
+            scales[qt] = work.tile([P, H * P], U8, tag="scales", bufs=2, name="scales", align_bytes=64)
+            nc.vector.quantize_mx(
+                out=codes[qt][:].bitcast(FP8X4),
+                scales=scales[qt][:],
+                in_=w[qt][:].rearrange("p h q j -> p (h q j)"),
+            )
+
+        def context(qt, part, tag="ctx", bufs=1):
+            ctx_ps[(qt, part)] = psum.tile([P, 4, DH], F32, tag=tag, bufs=bufs, name="ctx_ps")
+            b = qt // QT_PER_B
             for i in range(4):
-                h = hh * 4 + i
+                cols = slice((4 * part + i) * P, (4 * part + i + 1) * P)
                 nc.tensor.matmul_mx(
-                    out=t[:, i, :],
-                    lhsT=codes[pair][:, h * P:(h + 1) * P].bitcast(FP8X4),
-                    lhsT_scale=planes[pair][:, h * P:(h + 1) * P],
-                    rhs=vcodes[:, b * DH:(b + 1) * DH].bitcast(FP8X4),
-                    rhs_scale=vplane[:, b * DH:(b + 1) * DH],
+                    out=ctx_ps[(qt, part)][:, i, :],
+                    lhsT=codes[qt][:, cols].bitcast(FP8X4),
+                    lhsT_scale=scales[qt][:, cols],
+                    rhs=v_codes[:, b * DH:(b + 1) * DH].bitcast(FP8X4),
+                    rhs_scale=v_scales[:, b * DH:(b + 1) * DH],
                     start=True,
                     stop=True,
                 )
 
-        def o_evac(pair, hh, last=False):
-            if hh == 0:
-                t = work.tile([P, H * DH], F32, tag="osb", bufs=2, name="osb")
-                osb[pair] = t
-            cols = slice(hh * 512, (hh + 1) * 512)
-            src = o[(pair, hh)][:].rearrange("p a c -> p (a c)")
-            b = pair // (NPAIR // B)
-            r0 = (pair % (NPAIR // B)) * P
-            if last and hh == 1:
-                nc.vector.tensor_copy(out=osb[pair][:, cols], in_=src)
-            else:
-                nc.scalar.copy(out=osb[pair][:, cols], in_=src)
-            if last:
-                nc.sync.dma_start(out=out[b, r0:r0 + P, cols], in_=osb[pair][:, cols])
-            elif hh == 1:
-                nc.sync.dma_start(out=out[b, r0:r0 + P, :], in_=osb[pair][:])
+        def copy_out(qt, part):
+            if part == 0:
+                out_sb[qt] = work.tile([P, H * DH], F32, tag="out_sb", bufs=2, name="out_sb")
+            nc.scalar.copy(
+                out=out_sb[qt][:, part * 4 * DH:(part + 1) * 4 * DH],
+                in_=ctx_ps[(qt, part)][:].rearrange("p a c -> p (a c)"),
+            )
+            if part == 1:
+                b, r = rows(qt)
+                nc.sync.dma_start(out=out[b, r, :], in_=out_sb[qt][:])
 
         load_q(0)
         for j in range(J):
             load_k(0, j)
-        load_q(1)
+        for qt in range(1, FIRST_LOADS):
+            load_q(qt)
         for b in range(B):
             nc.sync.dma_start(
-                out=vraw[:, b, :, :], in_=value[b].rearrange("(p j) d -> p j d", j=J)
+                out=v_raw[:, b, :, :], in_=value[b].rearrange("(p j) d -> p j d", j=J)
             )
-        make_identity(nc, identb[:])
-        make_identity(nc, identf[:])
-        q_transpose(0)
-        k_transpose(0, 0, "st", 1)
-        k_transpose(0, 1, "lb", 1)
-        k_transpose(0, 2, "o", 1)
-        q_evac(0)
-        k_transpose(0, 3, "tp", 1)
+        make_identity(nc, ident_bf[:])
+        make_identity(nc, ident_f[:])
+        transpose_heads(("q", 0), q_raw[0], "tr")
+        for j, tag in enumerate(["sum", "log", "ctx"]):
+            transpose_heads(("k", 0, j), k_raw[0][:, j, :], tag)
+        copy_q(0)
+        transpose_heads(("k", 0, 3), k_raw[0][:, 3, :], "tr")
         for j in range(J):
-            k_evac(0, j)
-            qk(0, j)
-        q_transpose(1)
-        q_evac(1)
-        nc.vector.tensor_copy(out=vg[:], in_=vraw[:].rearrange("p b j d -> p b d j"))
+            copy_k(0, j)
+            scores(0, j)
+        transpose_heads(("q", 1), q_raw[1], "tr")
+        copy_q(1)
+        nc.vector.tensor_copy(out=v_words[:], in_=v_raw[:].rearrange("p b j d -> p b d j"))
         nc.vector.quantize_mx(
-            out=vcodes[:].bitcast(FP8X4),
-            scales=vplane[:],
-            in_=vg[:].rearrange("p b d j -> p (b d j)"),
+            out=v_codes[:].bitcast(FP8X4),
+            scales=v_scales[:],
+            in_=v_words[:].rearrange("p b d j -> p (b d j)"),
         )
 
-        for tau in range(NBLK):
-            for qt in ldq_at.get(tau, []):
-                load_q(qt)
-            for j in ldk_at.get(tau, []):
-                load_k(1, j)
-            for pair in lb_at.get(tau, []):
-                l_back(pair)
-            if 0 <= tau - 2 < NBLK:
-                sumt(tau - 2)
-            for pair, hh in oe_at.get(tau, []):
-                o_evac(pair, hh)
-            for qt in qte_at.get(tau, []):
-                q_evac(qt)
-            for j in kte_at.get(tau, []):
-                k_evac(1, j)
-            for pair in lb_at.get(tau, []):
-                rexp(pair)
-            if 0 <= tau - 1 < NBLK:
-                expo(tau - 1)
-            has = tau < NBLK
-            nxt = tau + 1 < NBLK
+        for step in range(N_HALF):
+            if due(step, LOAD_Q) >= FIRST_LOADS:
+                load_q(due(step, LOAD_Q))
+            if step < J:
+                load_k(1, step)
 
-            def slot(i):
-                if i == QPOS:
-                    for pair in qz_at.get(tau, []):
-                        quant(pair)
-                    for g in mul_at.get(tau, []):
-                        mul(g)
-                if i == 1:
-                    for pair, hh in mx_at.get(tau, []):
-                        mx(pair, hh)
-                if i == 2:
-                    for qt in qtt_at.get(tau, []):
-                        q_transpose(qt)
-                    for j in ktt_at.get(tau, []):
-                        k_transpose(1, j, "tp", 1)
+            group, i = divmod(step - WEIGHTS, 2 * GROUP)
+            back = GROUP * group + i if group >= 0 and i < GROUP else -1
+            if back >= 0:
+                log_back(back)
+            if step >= 2:
+                head_sum(step - 2)
 
-            slot(0)
-            if has:
-                red(tau, 0)
-                red(tau, 1)
-                sub(tau, 0)
-            if nxt:
-                qk(tau + 1, 0)
-            slot(1)
-            if has:
-                red(tau, 2)
-                sub(tau, 1)
-            if nxt:
-                qk(tau + 1, 1)
-            slot(2)
-            if has:
-                red(tau, 3)
-                sub(tau, 2)
-            if nxt:
-                qk(tau + 1, 2)
-            slot(3)
-            if has:
-                sub(tau, 3)
-            if nxt:
-                qk(tau + 1, 3)
-            slot(4)
-            if 0 <= tau - 2 < NBLK and (tau - 2) % 2 == 1:
-                st_evac((tau - 2) // 2)
-            for gi in ln_at.get(tau, []):
-                ln(gi)
+            if 0 <= due(step, COPY_OUT) < QT_VECTOR:
+                copy_out(due(step, COPY_OUT), 0)
+            if 0 <= due(step, COPY_OUT + 1) < QT_VECTOR:
+                copy_out(due(step, COPY_OUT + 1), 1)
+            if due(step, COPY_Q) >= 2:
+                copy_q(due(step, COPY_Q))
+            if K1_FIRST < step <= K1_FIRST + 2 * J and (step - K1_FIRST) % 2 == 1:
+                copy_k(1, (step - K1_FIRST) // 2)
+            if back >= 0:
+                inverse(back)
+            if step >= 1:
+                exponent(step - 1)
 
-        def mul_quant(pair):
-            mul(2 * pair)
-            mul(2 * pair + 1)
-            quant(pair)
+            head_max(step, 0)
+            head_max(step, 1)
+            shift(step, 0)
+            if step + 1 < N_HALF:
+                scores(step + 1, 0)
+            if 0 <= due(step, CONTEXT) < QT_VECTOR:
+                context(due(step, CONTEXT), 0)
+            if 0 <= due(step, CONTEXT + 1) < QT_VECTOR:
+                context(due(step, CONTEXT + 1), 1)
+            head_max(step, 2)
+            shift(step, 1)
+            if step + 1 < N_HALF:
+                scores(step + 1, 1)
+            if due(step, TRANSPOSE_Q) >= 2:
+                transpose_heads(("q", due(step, TRANSPOSE_Q)), q_raw[due(step, TRANSPOSE_Q)], "tr")
+            if K1_FIRST <= step < K1_FIRST + 2 * J and (step - K1_FIRST) % 2 == 0:
+                j = (step - K1_FIRST) // 2
+                transpose_heads(("k", 1, j), k_raw[1][:, j, :], "tr")
+            head_max(step, 3)
+            shift(step, 2)
+            if step + 1 < N_HALF:
+                scores(step + 1, 2)
+            shift(step, 3)
+            if step + 1 < N_HALF:
+                scores(step + 1, 3)
 
-        def mx_both(pair):
-            mx(pair, 0, "s", 4)
-            mx(pair, 1, "s", 4)
+            if 0 <= due(step, QUANTISE) < QT_VECTOR:
+                quantise(due(step, QUANTISE))
+            if 0 <= due(step, WEIGHTS) < QT_VECTOR:
+                weights(due(step, WEIGHTS), nc.gpsimd)
 
-        def evac_both(pair):
-            o_evac(pair, 0)
-            o_evac(pair, 1)
+            if step >= 3 and step % 2 == 1:
+                copy_sum((step - 2) // 2)
+                if ((step - 2) // 2) % GROUP == GROUP - 1:
+                    log_sum((step - 2) // 2 // GROUP, GROUP)
 
-        pv = (FIRST_V + 1) // 2
-        assert FIRST_V % 2 == 1 and last_step == NBLK + 1 and GROUPS[-1] == 3 and pv <= NPAIR - 4
-        o_evac(pv - 2, 0)
-        mx(pv - 2, 1)
-        sumt(NBLK - 2)
-        expo(NBLK - 1)
-        mul(FIRST_V)
-        quant(pv - 1)
-        mul_quant(pv)
-        sumt(NBLK - 1)
-        o_evac(pv - 2, 1)
-        mx_both(pv - 1)
-        ln_end()
-        l_back(NPAIR - 3, "lb")
-        l_back(NPAIR - 2, "tp")
-        rexp(NPAIR - 3)
-        l_back(NPAIR - 1, "lb")
-        rexp(NPAIR - 2)
-        rexp(NPAIR - 1)
-        evac_both(pv - 1)
-        mx_both(pv)
-        for pair in range(pv + 1, NPAIR):
-            mul_quant(pair)
-            evac_both(pair - 1)
-            mx_both(pair)
-        o_evac(NPAIR - 1, 0, True)
-        o_evac(NPAIR - 1, 1, True)
+        def finish(qt):
+            weights(qt, nc.vector)
+            quantise(qt)
+
+        def context_both(qt):
+            context(qt, 0, "s", 4)
+            context(qt, 1, "s", 4)
+
+        def copy_out_both(qt):
+            copy_out(qt, 0)
+            copy_out(qt, 1)
+
+        last = N_QT - 1
+        assert 2 * (QT_VECTOR - 1) + CONTEXT == N_HALF - 1
+        assert N_QT % GROUP == 2 and QT_VECTOR == GROUP * (N_QT // GROUP) - GROUP
+        copy_out(QT_VECTOR - 1, 0)
+        context(QT_VECTOR - 1, 1)
+        log_back(last - 2)
+        inverse(last - 2)
+        head_sum(N_HALF - 2)
+        exponent(N_HALF - 1)
+        finish(QT_VECTOR)
+        head_sum(N_HALF - 1)
+        copy_out(QT_VECTOR - 1, 1)
+        log_sum(last // GROUP, 1)
+        nc.scalar.activation(out=logT[last // GROUP][:, 1, :, :], in_=sumT[last][:], func=ACT.Ln)
+        log_back(last - 1, "log")
+        log_back(last, "tr")
+        inverse(last - 1)
+        inverse(last)
+        context_both(QT_VECTOR)
+        for qt in range(QT_VECTOR + 1, N_QT):
+            finish(qt)
+            copy_out_both(qt - 1)
+            context_both(qt)
+        copy_out_both(last)

@@ -129,8 +129,8 @@ def tile_multiheadattention_pa_t_kernel(tc, query, k, value, out):
             if hf % 2 == 0:
                 e[hf // 2] = work.tile([P, 2, H, HALF, J], F32, tag="e", bufs=6, name="e")
             nc.scalar.activation(
-                out=e[hf // 2][:, hf % 2, :, :, :],
-                in_=x[hf][:].rearrange("p j h q -> p h q j"),
+                out=e[hf // 2][:, hf % 2, :, :, :].rearrange("p h (c i) j -> p (h c) j i", i=4),
+                in_=x[hf][:].rearrange("p j h (c i) -> p (h c) j i", i=4),
                 func=ACT.Exp,
                 scale=SCALE,
             )

@@ -25,7 +25,8 @@ WORD_COLS = HALF * J
 SCALE = DH ** -0.5
 
 GROUP = 3
-QT_VECTOR = N_QT - 5
+QT_TAIL = N_QT - 5
+VECTOR_QT = (N_QT - 4, N_QT - 2, N_QT - 1)
 
 LOAD_Q = -7
 TRANSPOSE_Q = -3
@@ -117,7 +118,7 @@ def tile_multiheadattention_pa_t_kernel(tc, query, k, value, out):
 
         def shift(hf, j):
             if j == 0:
-                x[hf] = work.tile([P, J, H, HALF], F32, tag="x", bufs=3, name="x")
+                x[hf] = work.tile([P, J, H, HALF], F32, tag="x", bufs=3, name="x", align_bytes=64)
             nc.vector.tensor_tensor(
                 out=x[hf][:, j, :, :],
                 in0=s[(hf, j)][:],
@@ -177,6 +178,21 @@ def tile_multiheadattention_pa_t_kernel(tc, query, k, value, out):
                 in_=log[qt][:].rearrange("p a c -> p (a c)"),
                 func=ACT.Exp,
                 scale=-1.0,
+            )
+
+        def inverse_turned(group, first, n_qt):
+            part = logT[group][:, first:first + n_qt, :, :]
+            nc.scalar.activation(out=part, in_=part, func=ACT.Exp, scale=-1.0)
+
+        def weights_vector(qt):
+            w[qt] = work.tile([P, H, P, J], BF16, tag="x", bufs=3, name="w", align_bytes=64)
+            nc.vector.tensor_tensor(
+                out=w[qt][:].rearrange("p h (a q) j -> p h a (q j)", a=2),
+                in0=e[qt][:].rearrange("p a h q j -> p h a (q j)"),
+                in1=log[qt][:].rearrange("p (a c) x -> p a (c x)", a=2).unsqueeze(1).to_broadcast(
+                    [P, H, 2, WORD_COLS]
+                ),
+                op=ALU.mult,
             )
 
         def weights(qt, engine):
@@ -259,20 +275,22 @@ def tile_multiheadattention_pa_t_kernel(tc, query, k, value, out):
 
             group, i = divmod(step - WEIGHTS, 2 * GROUP)
             back = GROUP * group + i if group >= 0 and i < GROUP else -1
+            if back in VECTOR_QT:
+                inverse_turned(back // GROUP, back % GROUP, 1)
             if back >= 0:
                 log_back(back)
             if step >= 2:
                 head_sum(step - 2)
 
-            if 0 <= due(step, COPY_OUT) < QT_VECTOR:
+            if 0 <= due(step, COPY_OUT) < QT_TAIL:
                 copy_out(due(step, COPY_OUT), 0)
-            if 0 <= due(step, COPY_OUT + 1) < QT_VECTOR:
+            if 0 <= due(step, COPY_OUT + 1) < QT_TAIL:
                 copy_out(due(step, COPY_OUT + 1), 1)
             if due(step, COPY_Q) >= 2:
                 copy_q(due(step, COPY_Q))
             if K1_FIRST < step <= K1_FIRST + 2 * J and (step - K1_FIRST) % 2 == 1:
                 copy_k(1, (step - K1_FIRST) // 2)
-            if back >= 0:
+            if back >= 0 and back not in VECTOR_QT:
                 inverse(back)
             if step >= 1:
                 exponent(step - 1)
@@ -282,9 +300,9 @@ def tile_multiheadattention_pa_t_kernel(tc, query, k, value, out):
             shift(step, 0)
             if step + 1 < N_HALF:
                 scores(step + 1, 0)
-            if 0 <= due(step, CONTEXT) < QT_VECTOR:
+            if 0 <= due(step, CONTEXT) < QT_TAIL:
                 context(due(step, CONTEXT), 0)
-            if 0 <= due(step, CONTEXT + 1) < QT_VECTOR:
+            if 0 <= due(step, CONTEXT + 1) < QT_TAIL:
                 context(due(step, CONTEXT + 1), 1)
             head_max(step, 2)
             shift(step, 1)
@@ -303,19 +321,15 @@ def tile_multiheadattention_pa_t_kernel(tc, query, k, value, out):
             if step + 1 < N_HALF:
                 scores(step + 1, 3)
 
-            if 0 <= due(step, QUANTISE) < QT_VECTOR:
+            if 0 <= due(step, QUANTISE) < QT_TAIL:
                 quantise(due(step, QUANTISE))
-            if 0 <= due(step, WEIGHTS) < QT_VECTOR:
+            if 0 <= due(step, WEIGHTS) <= QT_TAIL:
                 weights(due(step, WEIGHTS), nc.gpsimd)
 
             if step >= 3 and step % 2 == 1:
                 copy_sum((step - 2) // 2)
                 if ((step - 2) // 2) % GROUP == GROUP - 1:
                     log_sum((step - 2) // 2 // GROUP, GROUP)
-
-        def finish(qt):
-            weights(qt, nc.vector)
-            quantise(qt)
 
         def context_both(qt):
             context(qt, 0, "s", 4)
@@ -326,26 +340,33 @@ def tile_multiheadattention_pa_t_kernel(tc, query, k, value, out):
             copy_out(qt, 1)
 
         last = N_QT - 1
-        assert 2 * (QT_VECTOR - 1) + CONTEXT == N_HALF - 1
-        assert N_QT % GROUP == 2 and QT_VECTOR == GROUP * (N_QT // GROUP) - GROUP
-        copy_out(QT_VECTOR - 1, 0)
-        context(QT_VECTOR - 1, 1)
-        log_back(last - 2)
-        inverse(last - 2)
+        assert 2 * (QT_TAIL - 1) + CONTEXT == N_HALF - 1
+        assert N_QT % GROUP == 2 and QT_TAIL == GROUP * (N_QT // GROUP) - GROUP
+        assert VECTOR_QT == (QT_TAIL + 1, last - 1, last)
+        copy_out(QT_TAIL - 1, 0)
+        context(QT_TAIL - 1, 1)
+        weights_vector(QT_TAIL + 1)
+        log_back(QT_TAIL + 2, "tr")
+        inverse(QT_TAIL + 2)
         head_sum(N_HALF - 2)
         exponent(N_HALF - 1)
-        finish(QT_VECTOR)
         head_sum(N_HALF - 1)
-        copy_out(QT_VECTOR - 1, 1)
+        copy_out(QT_TAIL - 1, 1)
+        quantise(QT_TAIL + 1)
+        quantise(QT_TAIL)
+        weights(QT_TAIL + 2, nc.gpsimd)
         log_sum(last // GROUP, 1)
         nc.scalar.activation(out=logT[last // GROUP][:, 1, :, :], in_=sumT[last][:], func=ACT.Ln)
-        log_back(last - 1, "log")
-        log_back(last, "tr")
-        inverse(last - 1)
-        inverse(last)
-        context_both(QT_VECTOR)
-        for qt in range(QT_VECTOR + 1, N_QT):
-            finish(qt)
-            copy_out_both(qt - 1)
+        inverse_turned(last // GROUP, 0, 2)
+        context_both(QT_TAIL + 1)
+        context_both(QT_TAIL)
+        log_back(last - 1, "ctx")
+        log_back(last, "sum")
+        copy_out_both(QT_TAIL + 1)
+        copy_out_both(QT_TAIL)
+        weights_vector(last - 1)
+        weights_vector(last)
+        for qt in (QT_TAIL + 2, last - 1, last):
+            quantise(qt)
             context_both(qt)
-        copy_out_both(last)
+            copy_out_both(qt)

@@ -239,6 +239,18 @@ def tile_multiheadattention_pa_t_kernel(tc, query, k, value, out):
                 b, r = rows(qt)
                 nc.sync.dma_start(out=out[b, r, :], in_=out_sb[qt][:])
 
+        def copy_out_split(qt):
+            out_sb[qt] = work.tile([P, H * DH], F32, tag="out_sb", bufs=2, name="out_sb")
+            b, r = rows(qt)
+            for part in range(2):
+                cols = slice(part * 4 * DH, (part + 1) * 4 * DH)
+                bank = ctx_ps[(qt, part)][:].rearrange("p a c -> p (a c)")
+                if part == 0:
+                    nc.scalar.copy(out=out_sb[qt][:, cols], in_=bank)
+                else:
+                    nc.vector.tensor_copy(out=out_sb[qt][:, cols], in_=bank)
+                nc.sync.dma_start(out=out[b, r, cols], in_=out_sb[qt][:, cols])
+
         load_q(0)
         for j in range(J):
             load_k(0, j)
@@ -351,22 +363,28 @@ def tile_multiheadattention_pa_t_kernel(tc, query, k, value, out):
         head_sum(N_HALF - 2)
         exponent(N_HALF - 1)
         head_sum(N_HALF - 1)
-        copy_out(QT_TAIL - 1, 1)
         quantise(QT_TAIL + 1)
         quantise(QT_TAIL)
         weights(QT_TAIL + 2, nc.gpsimd)
         log_sum(last // GROUP, 1)
         nc.scalar.activation(out=logT[last // GROUP][:, 1, :, :], in_=sumT[last][:], func=ACT.Ln)
-        inverse_turned(last // GROUP, 0, 2)
+        inverse_turned(last // GROUP, 0, 1)
+        inverse_turned(last // GROUP, 1, 1)
+        copy_out(QT_TAIL - 1, 1)
         context_both(QT_TAIL + 1)
         context_both(QT_TAIL)
-        log_back(last - 1, "ctx")
+        log_back(last - 1, "log")
         log_back(last, "sum")
         copy_out_both(QT_TAIL + 1)
         copy_out_both(QT_TAIL)
         weights_vector(last - 1)
         weights_vector(last)
-        for qt in (QT_TAIL + 2, last - 1, last):
-            quantise(qt)
-            context_both(qt)
-            copy_out_both(qt)
+        quantise(QT_TAIL + 2)
+        context_both(QT_TAIL + 2)
+        quantise(last - 1)
+        context_both(last - 1)
+        copy_out_both(QT_TAIL + 2)
+        quantise(last)
+        context_both(last)
+        copy_out_split(last - 1)
+        copy_out_split(last)

@@ -118,7 +118,7 @@ def tile_multiheadattention_pa_t_kernel(tc, query, k, value, out):
 
         def shift(hf, j):
             if j == 0:
-                x[hf] = work.tile([P, J, H, HALF], F32, tag="x", bufs=3, name="x", align_bytes=64)
+                x[hf] = work.tile([P, J, H, HALF], F32, tag="x", bufs=4, name="x", align_bytes=64)
             nc.vector.tensor_tensor(
                 out=x[hf][:, j, :, :],
                 in0=s[(hf, j)][:],
@@ -185,7 +185,7 @@ def tile_multiheadattention_pa_t_kernel(tc, query, k, value, out):
             nc.scalar.activation(out=part, in_=part, func=ACT.Exp, scale=-1.0)
 
         def weights_vector(qt):
-            w[qt] = work.tile([P, H, P, J], BF16, tag="x", bufs=3, name="w", align_bytes=64)
+            w[qt] = work.tile([P, H, P, J], BF16, tag="x", bufs=4, name="w", align_bytes=64)
             nc.vector.tensor_tensor(
                 out=w[qt][:].rearrange("p h (a q) j -> p h a (q j)", a=2),
                 in0=e[qt][:].rearrange("p a h q j -> p h a (q j)"),
@@ -205,8 +205,8 @@ def tile_multiheadattention_pa_t_kernel(tc, query, k, value, out):
             )
 
         def quantise(qt):
-            codes[qt] = work.tile([P, H * P], U32, tag="codes", bufs=2, name="codes", align_bytes=64)
-            scales[qt] = work.tile([P, H * P], U8, tag="scales", bufs=2, name="scales", align_bytes=64)
+            codes[qt] = work.tile([P, H * P], U32, tag="codes", bufs=3, name="codes", align_bytes=64)
+            scales[qt] = work.tile([P, H * P], U8, tag="scales", bufs=3, name="scales", align_bytes=64)
             nc.vector.quantize_mx(
                 out=codes[qt][:].bitcast(FP8X4),
                 scales=scales[qt][:],
@@ -230,7 +230,7 @@ def tile_multiheadattention_pa_t_kernel(tc, query, k, value, out):
 
         def copy_out(qt, part):
             if part == 0:
-                out_sb[qt] = work.tile([P, H * DH], F32, tag="out_sb", bufs=2, name="out_sb")
+                out_sb[qt] = work.tile([P, H * DH], F32, tag="out_sb", bufs=3, name="out_sb")
             nc.scalar.copy(
                 out=out_sb[qt][:, part * 4 * DH:(part + 1) * 4 * DH],
                 in_=ctx_ps[(qt, part)][:].rearrange("p a c -> p (a c)"),
@@ -240,7 +240,7 @@ def tile_multiheadattention_pa_t_kernel(tc, query, k, value, out):
                 nc.sync.dma_start(out=out[b, r, :], in_=out_sb[qt][:])
 
         def copy_out_split(qt):
-            out_sb[qt] = work.tile([P, H * DH], F32, tag="out_sb", bufs=2, name="out_sb")
+            out_sb[qt] = work.tile([P, H * DH], F32, tag="out_sb", bufs=3, name="out_sb")
             b, r = rows(qt)
             for part in range(2):
                 cols = slice(part * 4 * DH, (part + 1) * 4 * DH)
@@ -339,9 +339,15 @@ def tile_multiheadattention_pa_t_kernel(tc, query, k, value, out):
                 weights(due(step, WEIGHTS), nc.gpsimd)
 
             if step >= 3 and step % 2 == 1:
-                copy_sum((step - 2) // 2)
                 if ((step - 2) // 2) % GROUP == GROUP - 1:
-                    log_sum((step - 2) // 2 // GROUP, GROUP)
+                    nc.scalar.activation(
+                        out=logT[(step - 2) // 2 // GROUP][:, GROUP - 1, :, :],
+                        in_=sumT[(step - 2) // 2][:],
+                        func=ACT.Ln,
+                    )
+                    log_sum((step - 2) // 2 // GROUP, GROUP - 1)
+                else:
+                    copy_sum((step - 2) // 2)
 
         def context_both(qt):
             context(qt, 0, "s", 4)

@@ -26,7 +26,7 @@ SCALE = DH ** -0.5
 
 GROUP = 3
 QT_TAIL = N_QT - 5
-VECTOR_QT = (N_QT - 4, N_QT - 2, N_QT - 1)
+VECTOR_QT = (N_QT - 4, N_QT - 3, N_QT - 2, N_QT - 1)
 
 LOAD_Q = -7
 TRANSPOSE_Q = -3
@@ -360,37 +360,37 @@ def tile_multiheadattention_pa_t_kernel(tc, query, k, value, out):
         last = N_QT - 1
         assert 2 * (QT_TAIL - 1) + CONTEXT == N_HALF - 1
         assert N_QT % GROUP == 2 and QT_TAIL == GROUP * (N_QT // GROUP) - GROUP
-        assert VECTOR_QT == (QT_TAIL + 1, last - 1, last)
+        assert VECTOR_QT == (QT_TAIL + 1, QT_TAIL + 2, last - 1, last)
         copy_out(QT_TAIL - 1, 0)
         context(QT_TAIL - 1, 1)
         weights_vector(QT_TAIL + 1)
+        inverse_turned((QT_TAIL + 2) // GROUP, (QT_TAIL + 2) % GROUP, 1)
         log_back(QT_TAIL + 2, "tr")
-        inverse(QT_TAIL + 2)
         head_sum(N_HALF - 2)
         exponent(N_HALF - 1)
         head_sum(N_HALF - 1)
-        quantise(QT_TAIL + 1)
+        weights_vector(QT_TAIL + 2)
         quantise(QT_TAIL)
-        weights(QT_TAIL + 2, nc.gpsimd)
+        quantise(QT_TAIL + 1)
+        quantise(QT_TAIL + 2)
         log_sum(last // GROUP, 1)
         nc.scalar.activation(out=logT[last // GROUP][:, 1, :, :], in_=sumT[last][:], func=ACT.Ln)
         inverse_turned(last // GROUP, 0, 1)
         inverse_turned(last // GROUP, 1, 1)
         copy_out(QT_TAIL - 1, 1)
-        context_both(QT_TAIL + 1)
         context_both(QT_TAIL)
+        context_both(QT_TAIL + 1)
         log_back(last - 1, "log")
         log_back(last, "sum")
-        copy_out_both(QT_TAIL + 1)
         copy_out_both(QT_TAIL)
-        weights_vector(last - 1)
-        weights_vector(last)
-        quantise(QT_TAIL + 2)
+        copy_out_both(QT_TAIL + 1)
         context_both(QT_TAIL + 2)
+        weights_vector(last - 1)
+        copy_out_both(QT_TAIL + 2)
         quantise(last - 1)
         context_both(last - 1)
-        copy_out_both(QT_TAIL + 2)
+        weights_vector(last)
+        copy_out_both(last - 1)
         quantise(last)
         context_both(last)
-        copy_out_split(last - 1)
         copy_out_split(last)

@@ -35,6 +35,7 @@ WEIGHTS = 2 * GROUP + 2
 QUANTISE = WEIGHTS + 2
 CONTEXT = QUANTISE + 1
 COPY_OUT = CONTEXT + 1
+H_SPLIT = 4
 K1_FIRST = 8
 FIRST_LOADS = 4
 
@@ -192,6 +193,28 @@ def tile_multiheadattention_pa_t_kernel(tc, query, k, value, out):
                 in1=log[qt][:].rearrange("p (a c) x -> p a (c x)", a=2).unsqueeze(1).to_broadcast(
                     [P, H, 2, WORD_COLS]
                 ),
+                op=ALU.mult,
+            )
+
+        def copy_inverse(qt):
+            inv[qt] = work.tile([P, 2, WORD_COLS], F32, tag="inv", bufs=4, name="inv")
+            nc.scalar.copy(
+                out=inv[qt][:].rearrange("p a c -> p (a c)"),
+                in_=log[qt][:].rearrange("p a c -> p (a c)"),
+            )
+
+        def weights_shared(qt, engine):
+            if qt not in w:
+                w[qt] = work.tile([P, H, P, J], BF16, tag="x", bufs=4, name="w", align_bytes=64)
+            if engine is nc.gpsimd:
+                heads, factor = slice(H_SPLIT, H), inv[qt][:]
+            else:
+                heads, factor = slice(0, H_SPLIT), log[qt][:].rearrange("p (a c) x -> p a (c x)", a=2)
+            n_heads = heads.stop - heads.start
+            engine.tensor_tensor(
+                out=w[qt][:].rearrange("p h (a q) j -> p h a (q j)", a=2)[:, heads],
+                in0=e[qt][:].rearrange("p a h q j -> p h a (q j)")[:, heads],
+                in1=factor.unsqueeze(1).to_broadcast([P, n_heads, 2, WORD_COLS]),
                 op=ALU.mult,
             )
 
@@ -385,12 +408,14 @@ def tile_multiheadattention_pa_t_kernel(tc, query, k, value, out):
         copy_out_both(QT_TAIL)
         copy_out_both(QT_TAIL + 1)
         context_both(QT_TAIL + 2)
+        copy_inverse(last)
+        weights_shared(last, nc.gpsimd)
         weights_vector(last - 1)
         copy_out_both(QT_TAIL + 2)
+        weights_shared(last, nc.vector)
         quantise(last - 1)
         context_both(last - 1)
-        weights_vector(last)
-        copy_out_both(last - 1)
         quantise(last)
+        copy_out_both(last - 1)
         context_both(last)
         copy_out_split(last)

from contextlib import ExitStack

import concourse.mybir as mybir
from concourse.masks import make_identity

F32 = mybir.dt.float32
BF16 = mybir.dt.bfloat16
U32 = mybir.dt.uint32
U8 = mybir.dt.uint8
FP8X4 = mybir.dt.float8_e4m3fn_x4
ACT = mybir.ActivationFunctionType
ALU = mybir.AluOpType
AX = mybir.AxisListType

B, TQ, TV, H, DH = 2, 2048, 512, 8, 128
FLOPS = 2 * 2 * B * H * TQ * TV * DH

P = 128
J = TV // P
HALF = 64
N_HALF = B * TQ // HALF
N_QT = N_HALF // 2
QT_PER_B = N_QT // B
WORD_COLS = HALF * J
SCALE = DH ** -0.5

GROUP = 3
QT_TAIL = N_QT - 5
VECTOR_QT = (N_QT - 4, N_QT - 3, N_QT - 2, N_QT - 1)

LOAD_Q = -7
TRANSPOSE_Q = -3
COPY_Q = -2
WEIGHTS = 2 * GROUP + 2
QUANTISE = WEIGHTS + 2
CONTEXT = QUANTISE + 1
COPY_OUT = CONTEXT + 1
H_SPLIT = 4
K1_FIRST = 8
FIRST_LOADS = 4


def due(step, offset):
    qt, odd = divmod(step - offset, 2)
    return qt if odd == 0 and 0 <= qt < N_QT else -1


def tile_multiheadattention_pa_t_kernel(tc, query, k, value, out):
    nc = tc.nc
    with ExitStack() as ctx:
        const = ctx.enter_context(tc.tile_pool(name="const", bufs=1))
        work = ctx.enter_context(tc.tile_pool(name="work", bufs=1))
        psum = ctx.enter_context(tc.psum_pool(name="psum", bufs=1))
        ctx.enter_context(tc.manual_schedule())

        ident_bf = const.tile([P, P], BF16, name="ident_bf")
        ident_f = const.tile([P, P], F32, name="ident_f")
        kT = [const.tile([P, J, H, P], BF16, name="kT%d" % b) for b in range(B)]
        v_raw = const.tile([P, B, J, DH], BF16, name="v_raw")
        v_words = const.tile([P, B, DH, J], BF16, name="v_words", align_bytes=64)
        v_codes = const.tile([P, B * DH], U32, name="v_codes", align_bytes=64)
        v_scales = const.tile([P, B * DH], U8, name="v_scales", align_bytes=64)

        k_raw, q_raw, turned, qT = {}, {}, {}, {}
        s, top, x, e = {}, {}, {}, {}
        sumT, logT, log, inv = {}, {}, {}, {}
        w, codes, scales, ctx_ps, out_sb = {}, {}, {}, {}, {}

        def rows(qt):
            return qt // QT_PER_B, slice((qt % QT_PER_B) * P, (qt % QT_PER_B + 1) * P)

        def load_k(b, j):
            if j == 0:
                k_raw[b] = work.tile([P, J, H * DH], BF16, tag="k_raw", name="k_raw")
            nc.sync.dma_start(
                out=k_raw[b][:, j, :], in_=k[b].rearrange("(p j) c -> p j c", j=J)[:, j, :]
            )

        def load_q(qt):
            b, r = rows(qt)
            q_raw[qt] = work.tile([P, H * DH], BF16, tag="q_raw", bufs=4, name="q_raw")
            nc.sync.dma_start(out=q_raw[qt][:], in_=query[b, r, :])

        def transpose_heads(key, src, tag):
            turned[key] = psum.tile([P, H, P], BF16, tag=tag, name="turned")
            for h in range(H):
                nc.tensor.transpose(
                    turned[key][:, h, :], src[:, h * DH:(h + 1) * DH], ident_bf[:]
                )

        def copy_k(b, j):
            nc.scalar.copy(out=kT[b][:, j, :, :], in_=turned[("k", b, j)][:])

        def copy_q(qt):
            qT[qt] = work.tile([P, H, P], BF16, tag="qT", bufs=3, name="qT")
            nc.scalar.copy(out=qT[qt][:], in_=turned[("q", qt)][:])

        def scores(hf, j):
            s[(hf, j)] = psum.tile([P, H, HALF], F32, tag="s", bufs=4, name="s")
            side = hf % 2
            for h in range(H):
                nc.tensor.matmul(
                    s[(hf, j)][:, h, :],
                    lhsT=kT[hf // (N_HALF // B)][:, j, h, :],
                    rhs=qT[hf // 2][:, h, side * HALF:(side + 1) * HALF],
                    start=True,
                    stop=True,
                )

        def head_max(hf, j):
            if j == 0:
                top[hf] = work.tile([P, J, HALF], F32, tag="top", bufs=3, name="top")
            nc.vector.tensor_reduce(
                out=top[hf][:, j, :],
                in_=s[(hf, j)][:].rearrange("p h q -> p q h"),
                axis=AX.X,
                op=ALU.max,
            )

        def shift(hf, j):
            if j == 0:
                x[hf] = work.tile([P, J, H, HALF], F32, tag="x", bufs=4, name="x", align_bytes=64)
            nc.vector.tensor_tensor(
                out=x[hf][:, j, :, :],
                in0=s[(hf, j)][:],
                in1=top[hf][:, j, :].unsqueeze(1).to_broadcast([P, H, HALF]),
                op=ALU.subtract,
            )

        def exponent(hf):
            if hf % 2 == 0:
                e[hf // 2] = work.tile([P, 2, H, HALF, J], F32, tag="e", bufs=6, name="e")
            nc.scalar.activation(
                out=e[hf // 2][:, hf % 2, :, :, :].rearrange("p h (c i) j -> p (h c) j i", i=4),
                in_=x[hf][:].rearrange("p j h (c i) -> p (h c) j i", i=4),
                func=ACT.Exp,
                scale=SCALE,
            )

        def head_sum(hf):
            qt, side = divmod(hf, 2)
            if side == 0:
                sumT[qt] = psum.tile([P, 4, P], F32, tag="sum", name="sumT")
            for c in range(2):
                for h in range(H):
                    nc.tensor.matmul(
                        sumT[qt][:, 2 * side + c, :],
                        lhsT=e[qt][:, side, h, c * 32:(c + 1) * 32, :].rearrange(
                            "p q j -> p (q j)"
                        ),
                        rhs=ident_f[:],
                        is_transpose=True,
                        start=(h == 0),
                        stop=(h == H - 1),
                    )

        def copy_sum(qt):
            if qt % GROUP == 0:
                logT[qt // GROUP] = work.tile(
                    [P, GROUP, 4, P], F32, tag="logT", bufs=2, name="logT"
                )
            nc.scalar.copy(out=logT[qt // GROUP][:, qt % GROUP, :, :], in_=sumT[qt][:])

        def log_sum(group, n_qt):
            part = logT[group][:, 0:n_qt, :, :]
            nc.scalar.activation(out=part, in_=part, func=ACT.Ln)

        def log_back(qt, tag="log"):
            log[qt] = psum.tile([P, 4, P], F32, tag=tag, name="log")
            for c in range(4):
                nc.tensor.transpose(
                    log[qt][:, c, :], logT[qt // GROUP][:, qt % GROUP, c, :], ident_f[:]
                )

        def inverse(qt):
            inv[qt] = work.tile([P, 2, WORD_COLS], F32, tag="inv", bufs=4, name="inv")
            nc.scalar.activation(
                out=inv[qt][:].rearrange("p a c -> p (a c)"),
                in_=log[qt][:].rearrange("p a c -> p (a c)"),
                func=ACT.Exp,
                scale=-1.0,
            )

        def inverse_turned(group, first, n_qt):
            part = logT[group][:, first:first + n_qt, :, :]
            nc.scalar.activation(out=part, in_=part, func=ACT.Exp, scale=-1.0)

        def weights_vector(qt):
            w[qt] = work.tile([P, H, P, J], BF16, tag="x", bufs=4, name="w", align_bytes=64)
            nc.vector.tensor_tensor(
                out=w[qt][:].rearrange("p h (a q) j -> p h a (q j)", a=2),
                in0=e[qt][:].rearrange("p a h q j -> p h a (q j)"),
                in1=log[qt][:].rearrange("p (a c) x -> p a (c x)", a=2).unsqueeze(1).to_broadcast(
                    [P, H, 2, WORD_COLS]
                ),
                op=ALU.mult,
            )

        def copy_inverse(qt):
            inv[qt] = work.tile([P, 2, WORD_COLS], F32, tag="inv", bufs=4, name="inv")
            nc.scalar.copy(
                out=inv[qt][:].rearrange("p a c -> p (a c)"),
                in_=log[qt][:].rearrange("p a c -> p (a c)"),
            )

        def weights_shared(qt, engine):
            if qt not in w:
                w[qt] = work.tile([P, H, P, J], BF16, tag="x", bufs=4, name="w", align_bytes=64)
            if engine is nc.gpsimd:
                heads, factor = slice(H_SPLIT, H), inv[qt][:]
            else:
                heads, factor = slice(0, H_SPLIT), log[qt][:].rearrange("p (a c) x -> p a (c x)", a=2)
            n_heads = heads.stop - heads.start
            engine.tensor_tensor(
                out=w[qt][:].rearrange("p h (a q) j -> p h a (q j)", a=2)[:, heads],
                in0=e[qt][:].rearrange("p a h q j -> p h a (q j)")[:, heads],
                in1=factor.unsqueeze(1).to_broadcast([P, n_heads, 2, WORD_COLS]),
                op=ALU.mult,
            )

        def weights(qt, engine):
            w[qt] = work.tile([P, H, P, J], BF16, tag="w", name="w", align_bytes=64)
            engine.tensor_tensor(
                out=w[qt][:].rearrange("p h (a q) j -> p h a (q j)", a=2),
                in0=e[qt][:].rearrange("p a h q j -> p h a (q j)"),
                in1=inv[qt][:].unsqueeze(1).to_broadcast([P, H, 2, WORD_COLS]),
                op=ALU.mult,
            )

        def quantise(qt):
            codes[qt] = work.tile([P, H * P], U32, tag="codes", bufs=3, name="codes", align_bytes=64)
            scales[qt] = work.tile([P, H * P], U8, tag="scales", bufs=3, name="scales", align_bytes=64)
            nc.vector.quantize_mx(
                out=codes[qt][:].bitcast(FP8X4),
                scales=scales[qt][:],
                in_=w[qt][:].rearrange("p h q j -> p (h q j)"),
            )

        def context(qt, part, tag="ctx", bufs=1):
            ctx_ps[(qt, part)] = psum.tile([P, 4, DH], F32, tag=tag, bufs=bufs, name="ctx_ps")
            b = qt // QT_PER_B
            for i in range(4):
                cols = slice((4 * part + i) * P, (4 * part + i + 1) * P)
                nc.tensor.matmul_mx(
                    out=ctx_ps[(qt, part)][:, i, :],
                    lhsT=codes[qt][:, cols].bitcast(FP8X4),
                    lhsT_scale=scales[qt][:, cols],
                    rhs=v_codes[:, b * DH:(b + 1) * DH].bitcast(FP8X4),
                    rhs_scale=v_scales[:, b * DH:(b + 1) * DH],
                    start=True,
                    stop=True,
                )

        def copy_out(qt, part):
            if part == 0:
                out_sb[qt] = work.tile([P, H * DH], F32, tag="out_sb", bufs=3, name="out_sb")
            nc.scalar.copy(
                out=out_sb[qt][:, part * 4 * DH:(part + 1) * 4 * DH],
                in_=ctx_ps[(qt, part)][:].rearrange("p a c -> p (a c)"),
            )
            if part == 1:
                b, r = rows(qt)
                nc.sync.dma_start(out=out[b, r, :], in_=out_sb[qt][:])

        def copy_out_split(qt):
            out_sb[qt] = work.tile([P, H * DH], F32, tag="out_sb", bufs=3, name="out_sb")
            b, r = rows(qt)
            for part in range(2):
                cols = slice(part * 4 * DH, (part + 1) * 4 * DH)
                bank = ctx_ps[(qt, part)][:].rearrange("p a c -> p (a c)")
                if part == 0:
                    nc.scalar.copy(out=out_sb[qt][:, cols], in_=bank)
                else:
                    nc.vector.tensor_copy(out=out_sb[qt][:, cols], in_=bank)
                nc.sync.dma_start(out=out[b, r, cols], in_=out_sb[qt][:, cols])

        load_q(0)
        for j in range(J):
            load_k(0, j)
        for qt in range(1, FIRST_LOADS):
            load_q(qt)
        for b in range(B):
            nc.sync.dma_start(
                out=v_raw[:, b, :, :], in_=value[b].rearrange("(p j) d -> p j d", j=J)
            )
        make_identity(nc, ident_bf[:])
        make_identity(nc, ident_f[:])
        transpose_heads(("q", 0), q_raw[0], "tr")
        for j, tag in enumerate(["sum", "log", "ctx"]):
            transpose_heads(("k", 0, j), k_raw[0][:, j, :], tag)
        copy_q(0)
        transpose_heads(("k", 0, 3), k_raw[0][:, 3, :], "tr")
        for j in range(J):
            copy_k(0, j)
            scores(0, j)
        transpose_heads(("q", 1), q_raw[1], "tr")
        copy_q(1)
        nc.vector.tensor_copy(out=v_words[:], in_=v_raw[:].rearrange("p b j d -> p b d j"))
        nc.vector.quantize_mx(
            out=v_codes[:].bitcast(FP8X4),
            scales=v_scales[:],
            in_=v_words[:].rearrange("p b d j -> p (b d j)"),
        )

        for step in range(N_HALF):
            if due(step, LOAD_Q) >= FIRST_LOADS:
                load_q(due(step, LOAD_Q))
            if step < J:
                load_k(1, step)

            group, i = divmod(step - WEIGHTS, 2 * GROUP)
            back = GROUP * group + i if group >= 0 and i < GROUP else -1
            if back in VECTOR_QT:
                inverse_turned(back // GROUP, back % GROUP, 1)
            if back >= 0:
                log_back(back)
            if step >= 2:
                head_sum(step - 2)

            if 0 <= due(step, COPY_OUT) < QT_TAIL:
                copy_out(due(step, COPY_OUT), 0)
            if 0 <= due(step, COPY_OUT + 1) < QT_TAIL:
                copy_out(due(step, COPY_OUT + 1), 1)
            if due(step, COPY_Q) >= 2:
                copy_q(due(step, COPY_Q))
            if K1_FIRST < step <= K1_FIRST + 2 * J and (step - K1_FIRST) % 2 == 1:
                copy_k(1, (step - K1_FIRST) // 2)
            if back >= 0 and back not in VECTOR_QT:
                inverse(back)
            if step >= 1:
                exponent(step - 1)

            head_max(step, 0)
            head_max(step, 1)
            shift(step, 0)
            if step + 1 < N_HALF:
                scores(step + 1, 0)
            if 0 <= due(step, CONTEXT) < QT_TAIL:
                context(due(step, CONTEXT), 0)
            if 0 <= due(step, CONTEXT + 1) < QT_TAIL:
                context(due(step, CONTEXT + 1), 1)
            head_max(step, 2)
            shift(step, 1)
            if step + 1 < N_HALF:
                scores(step + 1, 1)
            if due(step, TRANSPOSE_Q) >= 2:
                transpose_heads(("q", due(step, TRANSPOSE_Q)), q_raw[due(step, TRANSPOSE_Q)], "tr")
            if K1_FIRST <= step < K1_FIRST + 2 * J and (step - K1_FIRST) % 2 == 0:
                j = (step - K1_FIRST) // 2
                transpose_heads(("k", 1, j), k_raw[1][:, j, :], "tr")
            head_max(step, 3)
            shift(step, 2)
            if step + 1 < N_HALF:
                scores(step + 1, 2)
            shift(step, 3)
            if step + 1 < N_HALF:
                scores(step + 1, 3)

            if 0 <= due(step, QUANTISE) < QT_TAIL:
                quantise(due(step, QUANTISE))
            if 0 <= due(step, WEIGHTS) <= QT_TAIL:
                weights(due(step, WEIGHTS), nc.gpsimd)

            if step >= 3 and step % 2 == 1:
                if ((step - 2) // 2) % GROUP == GROUP - 1:
                    nc.scalar.activation(
                        out=logT[(step - 2) // 2 // GROUP][:, GROUP - 1, :, :],
                        in_=sumT[(step - 2) // 2][:],
                        func=ACT.Ln,
                    )
                    log_sum((step - 2) // 2 // GROUP, GROUP - 1)
                else:
                    copy_sum((step - 2) // 2)

        def context_both(qt):
            context(qt, 0, "s", 4)
            context(qt, 1, "s", 4)

        def copy_out_both(qt):
            copy_out(qt, 0)
            copy_out(qt, 1)

        last = N_QT - 1
        assert 2 * (QT_TAIL - 1) + CONTEXT == N_HALF - 1
        assert N_QT % GROUP == 2 and QT_TAIL == GROUP * (N_QT // GROUP) - GROUP
        assert VECTOR_QT == (QT_TAIL + 1, QT_TAIL + 2, last - 1, last)
        copy_out(QT_TAIL - 1, 0)
        context(QT_TAIL - 1, 1)
        weights_vector(QT_TAIL + 1)
        inverse_turned((QT_TAIL + 2) // GROUP, (QT_TAIL + 2) % GROUP, 1)
        log_back(QT_TAIL + 2, "tr")
        head_sum(N_HALF - 2)
        exponent(N_HALF - 1)
        head_sum(N_HALF - 1)
        weights_vector(QT_TAIL + 2)
        quantise(QT_TAIL)
        quantise(QT_TAIL + 1)
        quantise(QT_TAIL + 2)
        log_sum(last // GROUP, 1)
        nc.scalar.activation(out=logT[last // GROUP][:, 1, :, :], in_=sumT[last][:], func=ACT.Ln)
        inverse_turned(last // GROUP, 0, 1)
        inverse_turned(last // GROUP, 1, 1)
        copy_out(QT_TAIL - 1, 1)
        context_both(QT_TAIL)
        context_both(QT_TAIL + 1)
        log_back(last - 1, "log")
        log_back(last, "sum")
        copy_out_both(QT_TAIL)
        copy_out_both(QT_TAIL + 1)
        context_both(QT_TAIL + 2)
        copy_inverse(last)
        weights_shared(last, nc.gpsimd)
        weights_vector(last - 1)
        copy_out_both(QT_TAIL + 2)
        weights_shared(last, nc.vector)
        quantise(last - 1)
        context_both(last - 1)
        quantise(last)
        copy_out_both(last - 1)
        context_both(last)
        copy_out_split(last)
